import numpy as np
import ml_dtypes


def mxq(x, axis, fmt="e4m3"):
    dtype, down = {"e4m3": (ml_dtypes.float8_e4m3fn, 7), "e5m2": (ml_dtypes.float8_e5m2, 14)}[fmt]
    v = np.moveaxis(np.asarray(x, np.float32).astype(ml_dtypes.bfloat16).astype(np.float64), axis, -1)
    blocks = v.reshape(v.shape[:-1] + (-1, 32))
    amax = np.abs(blocks).max(-1, keepdims=True)
    byte = np.maximum(np.where(amax > 0, np.frexp(amax)[1] - 1 + 127, 0) - down, 1)
    scale = np.exp2(byte - 127.0)
    codes = (blocks / scale).astype(np.float32).astype(dtype).astype(np.float64)
    return np.moveaxis((codes * scale).reshape(v.shape), -1, axis)


WIDE = False


def mx_kscale(k):
    if not WIDE:
        return np.ones(k)
    levels = np.array([20, -20, 10, -10, 0])
    a = np.random.permutation(np.resize(levels, k // 512 * 4)).reshape(k // 512, 4)
    idx = np.arange(k)
    return np.exp2(a[idx // 512, idx % 128 // 32])


BF16 = ml_dtypes.bfloat16


def bf(x):
    return np.asarray(x, np.float32).astype(BF16)


def f64(x):
    return np.asarray(x).astype(np.float64)


B, N, D, C = 2560, 1536, 1024, 8

SIGMA = 1.0


def setup_inputs():
    centres = (0.8 * np.random.standard_normal((1, D)) + 0.9 * np.random.standard_normal((C, D))) / np.sqrt(D)

    def draw(rows):
        amp = 0.5 + np.random.random((rows, 1))
        return bf(centres[np.random.randint(0, C, rows)] * amp + np.random.standard_normal((rows, D)) * 0.7 / np.sqrt(D))

    s = mx_kscale(B)
    sd = np.minimum(s, 1.0 / s)[:, None]
    x0 = draw(B)
    t = draw(N)
    g = bf(np.random.standard_normal((B, N)) * np.exp2(np.random.randint(-12, 1, (B, 1))) * 16.0 * sd)
    xf, tf = f64(x0), f64(t)
    dist = np.sum(xf * xf, axis=-1, keepdims=True) + np.sum(tf * tf, axis=-1)[None, :] - 2.0 * (xf @ tf.T)
    return {"inputs": bf(xf / sd), "train_data": t, "dist": np.asarray(dist, np.float32), "grad_out": g}


def reference(inputs, train_data, dist, grad_out):
    x, t, r = f64(inputs), f64(train_data), f64(dist)
    p = np.exp(-np.maximum(r, 0.0) / (2.0 * SIGMA ** 2))
    e = f64(grad_out) * p * (r > 0.0) / SIGMA ** 2
    col = np.sum(e, axis=0)
    m = mxq(e, 0, "e5m2").T @ mxq(x, 0, "e4m3")
    return m - t * col[:, None]

@@ -1,0 +1,157 @@
+from contextlib import ExitStack
+
+import concourse.mybir as mybir
+
+F32 = mybir.dt.float32
+BF16 = mybir.dt.bfloat16
+U32 = mybir.dt.uint32
+U8 = mybir.dt.uint8
+E4M3X4 = mybir.dt.float8_e4m3fn_x4
+E5M2X4 = mybir.dt.float8_e5m2_x4
+ALU = mybir.AluOpType
+EXP = mybir.ActivationFunctionType.Exp
+
+TOKENS, PATTERNS, FEATURES = 2560, 1536, 1024
+FLOPS = 2 * TOKENS * PATTERNS * FEATURES
+
+P = 128
+PACK = 4
+K_PASS = P * PACK
+PASSES = TOKENS // K_PASS
+BLOCK = 384
+N_TILES = BLOCK // P
+BLOCKS = PATTERNS // BLOCK
+HALF = 512
+HALVES = FEATURES // HALF
+RUN = 4
+COL_COPIES = 32
+
+
+def regroup(copy, grouped, rows):
+    copy(
+        out=grouped.rearrange("p (q i) j -> p q j i", i=RUN),
+        in_=rows.rearrange("p j (q i) -> p q j i", i=RUN),
+    )
+
+
+def tile_patternlayer_v_kernel(tc, inputs, train_data, dist, grad_out, out):
+    nc = tc.nc
+    with ExitStack() as ctx:
+        keep = ctx.enter_context(tc.tile_pool(name="keep", bufs=1))
+        loads = ctx.enter_context(tc.tile_pool(name="loads", bufs=4))
+        work = ctx.enter_context(tc.tile_pool(name="work", bufs=3))
+        coded = ctx.enter_context(tc.tile_pool(name="coded", bufs=8))
+        x_stage = ctx.enter_context(tc.tile_pool(name="x_stage", bufs=2))
+        t_pool = ctx.enter_context(tc.tile_pool(name="t_pool", bufs=2))
+        results = ctx.enter_context(tc.tile_pool(name="results", bufs=3))
+        acc_pool = ctx.enter_context(tc.psum_pool(name="acc_pool", bufs=7))
+        col_pool = ctx.enter_context(tc.psum_pool(name="col_pool", bufs=1))
+
+        neg_ones = keep.tile([P, COL_COPIES], F32)
+        nc.vector.memset(neg_ones[:], -1.0)
+        x_codes = keep.tile([P, PASSES, FEATURES], U32, align_bytes=64)
+        x_scales = keep.tile([P, PASSES, FEATURES], U8, align_bytes=64)
+
+        for blk in range(BLOCKS):
+            n0 = blk * BLOCK
+            acc = [
+                [acc_pool.tile([P, HALF], F32, name="acc_%d_%d" % (t, h), tag="acc") for h in range(HALVES)]
+                for t in range(N_TILES)
+            ]
+            col_ps = col_pool.tile([P, HALF], F32)
+            t_sb = t_pool.tile([P, N_TILES, FEATURES], BF16)
+
+            for c in range(PASSES):
+                rows = slice(c * K_PASS, (c + 1) * K_PASS)
+                r = loads.tile([P, PACK, BLOCK], F32)
+                nc.sync.dma_start(out=r[:], in_=dist[rows, n0 : n0 + BLOCK].rearrange("(p j) n -> p j n", j=PACK))
+                g = loads.tile([P, PACK, BLOCK], BF16)
+                nc.sync.dma_start(out=g[:], in_=grad_out[rows, n0 : n0 + BLOCK].rearrange("(p j) n -> p j n", j=PACK))
+
+                if blk == 0:
+                    x_raw = x_stage.tile([P, PACK, FEATURES], BF16)
+                    nc.sync.dma_start(out=x_raw[:], in_=inputs[rows, :].rearrange("(p j) d -> p j d", j=PACK))
+                    for h in range(HALVES):
+                        d_cols = slice(h * HALF, (h + 1) * HALF)
+                        x_grp = x_stage.tile([P, HALF, PACK], BF16, align_bytes=64, bufs=4)
+                        regroup(nc.scalar.copy if h == 0 else nc.vector.tensor_copy, x_grp[:], x_raw[:, :, d_cols])
+                        nc.vector.quantize_mx(
+                            out=x_codes[:, c, d_cols].bitcast(E4M3X4),
+                            scales=x_scales[:, c, d_cols],
+                            in_=x_grp[:].rearrange("p d j -> p (d j)"),
+                        )
+                if c == 0:
+                    nc.sync.dma_start(
+                        out=t_sb[:], in_=train_data[n0 : n0 + BLOCK, :].rearrange("(t p) d -> p t d", p=P)
+                    )
+
+                prob = work.tile([P, PACK, BLOCK], F32)
+                nc.scalar.activation(out=prob[:], in_=r[:], func=EXP, scale=-0.5)
+                g_kept = work.tile([P, PACK, BLOCK], BF16)
+                nc.vector.scalar_tensor_tensor(
+                    out=g_kept[:], in0=r[:], scalar=0.0, in1=g[:], op0=ALU.is_gt, op1=ALU.mult
+                )
+                e32 = work.tile([P, PACK, BLOCK], F32)
+                nc.vector.scalar_tensor_tensor(
+                    out=e32[:], in0=prob[:], scalar=1.0, in1=g_kept[:], op0=ALU.min, op1=ALU.mult
+                )
+
+                for t in range(N_TILES):
+                    first = (t * PASSES + c) * COL_COPIES
+                    for j in range(PACK):
+                        nc.tensor.matmul(
+                            out=col_ps[:, first : first + COL_COPIES],
+                            lhsT=e32[:, j, t * P : (t + 1) * P],
+                            rhs=neg_ones[:],
+                            start=(j == 0),
+                            stop=(j == PACK - 1),
+                        )
+
+                e16 = work.tile([P, BLOCK, PACK], BF16, align_bytes=64)
+                regroup(nc.scalar.copy, e16[:], e32[:])
+                e_codes = coded.tile([P, BLOCK], U32, align_bytes=64)
+                e_scales = coded.tile([P, BLOCK], U8, align_bytes=64)
+                for t in range(N_TILES):
+                    n_cols = slice(t * P, (t + 1) * P)
+                    nc.vector.quantize_mx(
+                        out=e_codes[:, n_cols].bitcast(E5M2X4),
+                        scales=e_scales[:, n_cols],
+                        in_=e16[:, n_cols, :].rearrange("p n j -> p (n j)"),
+                    )
+                for t in range(N_TILES):
+                    n_cols = slice(t * P, (t + 1) * P)
+                    for h in range(HALVES):
+                        d_cols = slice(h * HALF, (h + 1) * HALF)
+                        nc.tensor.matmul_mx(
+                            out=acc[t][h][:],
+                            lhsT=e_codes[:, n_cols].bitcast(E5M2X4),
+                            lhsT_scale=e_scales[:, n_cols],
+                            rhs=x_codes[:, c, d_cols].bitcast(E4M3X4),
+                            rhs_scale=x_scales[:, c, d_cols],
+                            start=(c == 0),
+                            stop=(c == PASSES - 1),
+                        )
+
+            neg_col = results.tile([P, N_TILES], F32)
+            nc.vector.tensor_reduce(
+                out=neg_col[:],
+                in_=col_ps[:, 0 : N_TILES * PASSES * COL_COPIES].rearrange(
+                    "p (t c k) -> p t c k", t=N_TILES, c=PASSES
+                )[:, :, :, 0],
+                axis=mybir.AxisListType.X,
+                op=ALU.add,
+            )
+            store_queue = nc.sync if blk == BLOCKS - 1 else nc.gpsimd
+            for t in range(N_TILES):
+                res = results.tile([P, FEATURES], F32)
+                for h in range(HALVES):
+                    d_cols = slice(h * HALF, (h + 1) * HALF)
+                    nc.vector.scalar_tensor_tensor(
+                        out=res[:, d_cols],
+                        in0=t_sb[:, t, d_cols],
+                        scalar=neg_col[:, t : t + 1],
+                        in1=acc[t][h][:],
+                        op0=ALU.mult,
+                        op1=ALU.add,
+                    )
+                store_queue.dma_start(out=out[n0 + t * P : n0 + (t + 1) * P, :], in_=res[:])

@@ -21,10 +21,15 @@ PASSES = TOKENS // K_PASS
 BLOCK = 384
 N_TILES = BLOCK // P
 BLOCKS = PATTERNS // BLOCK
+CHUNKS = BLOCKS * PASSES
 HALF = 512
 HALVES = FEATURES // HALF
 RUN = 4
 COL_COPIES = 32
+AHEAD = 2
+LOAD_BUFS = 5
+LOAD_AHEAD = LOAD_BUFS + AHEAD - 1
+X_BUFS = 3
 
 
 def regroup(copy, grouped, rows):
@@ -38,120 +43,177 @@ def tile_patternlayer_v_kernel(tc, inputs, train_data, dist, grad_out, out):
     nc = tc.nc
     with ExitStack() as ctx:
         keep = ctx.enter_context(tc.tile_pool(name="keep", bufs=1))
-        loads = ctx.enter_context(tc.tile_pool(name="loads", bufs=4))
+        loads = ctx.enter_context(tc.tile_pool(name="loads", bufs=LOAD_BUFS))
         work = ctx.enter_context(tc.tile_pool(name="work", bufs=3))
-        coded = ctx.enter_context(tc.tile_pool(name="coded", bufs=8))
-        x_stage = ctx.enter_context(tc.tile_pool(name="x_stage", bufs=2))
+        coded = ctx.enter_context(tc.tile_pool(name="coded", bufs=4))
+        x_stage = ctx.enter_context(tc.tile_pool(name="x_stage", bufs=X_BUFS))
         t_pool = ctx.enter_context(tc.tile_pool(name="t_pool", bufs=2))
-        results = ctx.enter_context(tc.tile_pool(name="results", bufs=3))
-        acc_pool = ctx.enter_context(tc.psum_pool(name="acc_pool", bufs=7))
-        col_pool = ctx.enter_context(tc.psum_pool(name="col_pool", bufs=1))
+        results = ctx.enter_context(tc.tile_pool(name="results", bufs=6))
+        acc_pool = ctx.enter_context(tc.psum_pool(name="acc_pool", bufs=N_TILES * HALVES))
+        col_pool = ctx.enter_context(tc.psum_pool(name="col_pool", bufs=2))
+        ctx.enter_context(tc.manual_schedule())
 
         neg_ones = keep.tile([P, COL_COPIES], F32)
         nc.vector.memset(neg_ones[:], -1.0)
         x_codes = keep.tile([P, PASSES, FEATURES], U32, align_bytes=64)
         x_scales = keep.tile([P, PASSES, FEATURES], U8, align_bytes=64)
 
-        for blk in range(BLOCKS):
-            n0 = blk * BLOCK
-            acc = [
-                [acc_pool.tile([P, HALF], F32, name="acc_%d_%d" % (t, h), tag="acc") for h in range(HALVES)]
-                for t in range(N_TILES)
-            ]
-            col_ps = col_pool.tile([P, HALF], F32)
-            t_sb = t_pool.tile([P, N_TILES, FEATURES], BF16)
+        r, g, prob, g_kept, e32, e16 = {}, {}, {}, {}, {}, {}
+        x_raw, x_grp, t_sb, col_ps, neg_col, acc = {}, {}, {}, {}, {}, {}
 
-            for c in range(PASSES):
-                rows = slice(c * K_PASS, (c + 1) * K_PASS)
-                r = loads.tile([P, PACK, BLOCK], F32)
-                nc.sync.dma_start(out=r[:], in_=dist[rows, n0 : n0 + BLOCK].rearrange("(p j) n -> p j n", j=PACK))
-                g = loads.tile([P, PACK, BLOCK], BF16)
-                nc.sync.dma_start(out=g[:], in_=grad_out[rows, n0 : n0 + BLOCK].rearrange("(p j) n -> p j n", j=PACK))
+        def load_chunk(i):
+            blk, c = divmod(i, PASSES)
+            rows = slice(c * K_PASS, (c + 1) * K_PASS)
+            cols = slice(blk * BLOCK, (blk + 1) * BLOCK)
+            r[i] = loads.tile([P, PACK, BLOCK], F32, name="r")
+            nc.sync.dma_start(out=r[i][:], in_=dist[rows, cols].rearrange("(p j) n -> p j n", j=PACK))
+            g[i] = loads.tile([P, PACK, BLOCK], BF16, name="g")
+            nc.sync.dma_start(out=g[i][:], in_=grad_out[rows, cols].rearrange("(p j) n -> p j n", j=PACK))
 
-                if blk == 0:
-                    x_raw = x_stage.tile([P, PACK, FEATURES], BF16)
-                    nc.sync.dma_start(out=x_raw[:], in_=inputs[rows, :].rearrange("(p j) d -> p j d", j=PACK))
-                    for h in range(HALVES):
-                        d_cols = slice(h * HALF, (h + 1) * HALF)
-                        x_grp = x_stage.tile([P, HALF, PACK], BF16, align_bytes=64, bufs=4)
-                        regroup(nc.scalar.copy if h == 0 else nc.vector.tensor_copy, x_grp[:], x_raw[:, :, d_cols])
-                        nc.vector.quantize_mx(
-                            out=x_codes[:, c, d_cols].bitcast(E4M3X4),
-                            scales=x_scales[:, c, d_cols],
-                            in_=x_grp[:].rearrange("p d j -> p (d j)"),
-                        )
-                if c == 0:
-                    nc.sync.dma_start(
-                        out=t_sb[:], in_=train_data[n0 : n0 + BLOCK, :].rearrange("(t p) d -> p t d", p=P)
-                    )
+        def load_x(c):
+            x_raw[c] = x_stage.tile([P, PACK, FEATURES], BF16, name="x_raw")
+            nc.sync.dma_start(
+                out=x_raw[c][:], in_=inputs[c * K_PASS : (c + 1) * K_PASS, :].rearrange("(p j) d -> p j d", j=PACK)
+            )
 
-                prob = work.tile([P, PACK, BLOCK], F32)
-                nc.scalar.activation(out=prob[:], in_=r[:], func=EXP, scale=-0.5)
-                g_kept = work.tile([P, PACK, BLOCK], BF16)
-                nc.vector.scalar_tensor_tensor(
-                    out=g_kept[:], in0=r[:], scalar=0.0, in1=g[:], op0=ALU.is_gt, op1=ALU.mult
-                )
-                e32 = work.tile([P, PACK, BLOCK], F32)
-                nc.vector.scalar_tensor_tensor(
-                    out=e32[:], in0=prob[:], scalar=1.0, in1=g_kept[:], op0=ALU.min, op1=ALU.mult
+        def load_patterns(blk):
+            t_sb[blk] = t_pool.tile([P, N_TILES, FEATURES], BF16, name="t_sb")
+            nc.sync.dma_start(
+                out=t_sb[blk][:],
+                in_=train_data[blk * BLOCK : (blk + 1) * BLOCK, :].rearrange("(t p) d -> p t d", p=P),
+            )
+
+        def mask_and_exp(i):
+            g_kept[i] = work.tile([P, PACK, BLOCK], BF16, name="g_kept")
+            nc.vector.scalar_tensor_tensor(
+                out=g_kept[i][:], in0=r[i][:], scalar=0.0, in1=g[i][:], op0=ALU.is_gt, op1=ALU.mult
+            )
+            prob[i] = work.tile([P, PACK, BLOCK], F32, name="prob")
+            nc.scalar.activation(out=prob[i][:], in_=r[i][:], func=EXP, scale=-0.5)
+
+        def regroup_x(c):
+            for h in range(HALVES):
+                x_grp[c, h] = x_stage.tile([P, HALF, PACK], BF16, name="x_grp", align_bytes=64, bufs=2 * HALVES)
+                regroup(
+                    nc.scalar.copy if h == 0 else nc.vector.tensor_copy,
+                    x_grp[c, h][:],
+                    x_raw[c][:, :, h * HALF : (h + 1) * HALF],
                 )
 
-                for t in range(N_TILES):
-                    first = (t * PASSES + c) * COL_COPIES
-                    for j in range(PACK):
-                        nc.tensor.matmul(
-                            out=col_ps[:, first : first + COL_COPIES],
-                            lhsT=e32[:, j, t * P : (t + 1) * P],
-                            rhs=neg_ones[:],
-                            start=(j == 0),
-                            stop=(j == PACK - 1),
-                        )
+        def quantise_x(c):
+            for h in range(HALVES):
+                d_cols = slice(h * HALF, (h + 1) * HALF)
+                nc.vector.quantize_mx(
+                    out=x_codes[:, c, d_cols].bitcast(E4M3X4),
+                    scales=x_scales[:, c, d_cols],
+                    in_=x_grp[c, h][:].rearrange("p d j -> p (d j)"),
+                )
 
-                e16 = work.tile([P, BLOCK, PACK], BF16, align_bytes=64)
-                regroup(nc.scalar.copy, e16[:], e32[:])
-                e_codes = coded.tile([P, BLOCK], U32, align_bytes=64)
-                e_scales = coded.tile([P, BLOCK], U8, align_bytes=64)
-                for t in range(N_TILES):
-                    n_cols = slice(t * P, (t + 1) * P)
-                    nc.vector.quantize_mx(
-                        out=e_codes[:, n_cols].bitcast(E5M2X4),
-                        scales=e_scales[:, n_cols],
-                        in_=e16[:, n_cols, :].rearrange("p n j -> p (n j)"),
+        def product(i):
+            blk, c = divmod(i, PASSES)
+            e32[i] = work.tile([P, PACK, BLOCK], F32, name="e32")
+            nc.vector.scalar_tensor_tensor(
+                out=e32[i][:], in0=prob[i][:], scalar=1.0, in1=g_kept[i][:], op0=ALU.min, op1=ALU.mult
+            )
+            if c == 0:
+                col_ps[blk] = col_pool.tile([P, HALF], F32, name="col_ps")
+            for t in range(N_TILES):
+                first = (t * PASSES + c) * COL_COPIES
+                for j in range(PACK):
+                    nc.tensor.matmul(
+                        out=col_ps[blk][:, first : first + COL_COPIES],
+                        lhsT=e32[i][:, j, t * P : (t + 1) * P],
+                        rhs=neg_ones[:],
+                        start=(j == 0),
+                        stop=(j == PACK - 1),
                     )
-                for t in range(N_TILES):
-                    n_cols = slice(t * P, (t + 1) * P)
-                    for h in range(HALVES):
-                        d_cols = slice(h * HALF, (h + 1) * HALF)
-                        nc.tensor.matmul_mx(
-                            out=acc[t][h][:],
-                            lhsT=e_codes[:, n_cols].bitcast(E5M2X4),
-                            lhsT_scale=e_scales[:, n_cols],
-                            rhs=x_codes[:, c, d_cols].bitcast(E4M3X4),
-                            rhs_scale=x_scales[:, c, d_cols],
-                            start=(c == 0),
-                            stop=(c == PASSES - 1),
-                        )
+            e16[i] = work.tile([P, BLOCK, PACK], BF16, name="e16", align_bytes=64)
+            for t in range(N_TILES):
+                n_cols = slice(t * P, (t + 1) * P)
+                regroup(nc.scalar.copy, e16[i][:, n_cols, :], e32[i][:, :, n_cols])
 
-            neg_col = results.tile([P, N_TILES], F32)
+        def quantise_and_multiply(i):
+            blk, c = divmod(i, PASSES)
+            if c == 0:
+                for t in range(N_TILES):
+                    for h in range(HALVES):
+                        acc[blk, t, h] = acc_pool.tile([P, HALF], F32, name="acc")
+            e_codes = coded.tile([P, BLOCK], U32, align_bytes=64)
+            e_scales = coded.tile([P, BLOCK], U8, align_bytes=64)
+            for t in range(N_TILES):
+                n_cols = slice(t * P, (t + 1) * P)
+                nc.vector.quantize_mx(
+                    out=e_codes[:, n_cols].bitcast(E5M2X4),
+                    scales=e_scales[:, n_cols],
+                    in_=e16[i][:, n_cols, :].rearrange("p n j -> p (n j)"),
+                )
+            for t in range(N_TILES):
+                n_cols = slice(t * P, (t + 1) * P)
+                for h in range(HALVES):
+                    d_cols = slice(h * HALF, (h + 1) * HALF)
+                    nc.tensor.matmul_mx(
+                        out=acc[blk, t, h][:],
+                        lhsT=e_codes[:, n_cols].bitcast(E5M2X4),
+                        lhsT_scale=e_scales[:, n_cols],
+                        rhs=x_codes[:, c, d_cols].bitcast(E4M3X4),
+                        rhs_scale=x_scales[:, c, d_cols],
+                        start=(c == 0),
+                        stop=(c == PASSES - 1),
+                    )
+
+        def sum_columns(blk):
+            neg_col[blk] = results.tile([P, N_TILES], F32, name="neg_col", bufs=2)
             nc.vector.tensor_reduce(
-                out=neg_col[:],
-                in_=col_ps[:, 0 : N_TILES * PASSES * COL_COPIES].rearrange(
+                out=neg_col[blk][:],
+                in_=col_ps[blk][:, 0 : N_TILES * PASSES * COL_COPIES].rearrange(
                     "p (t c k) -> p t c k", t=N_TILES, c=PASSES
                 )[:, :, :, 0],
                 axis=mybir.AxisListType.X,
                 op=ALU.add,
             )
-            store_queue = nc.sync if blk == BLOCKS - 1 else nc.gpsimd
+
+        def finish_block(blk):
             for t in range(N_TILES):
-                res = results.tile([P, FEATURES], F32)
+                n_rows = slice(blk * BLOCK + t * P, blk * BLOCK + (t + 1) * P)
                 for h in range(HALVES):
                     d_cols = slice(h * HALF, (h + 1) * HALF)
+                    res = results.tile([P, HALF], F32)
                     nc.vector.scalar_tensor_tensor(
-                        out=res[:, d_cols],
-                        in0=t_sb[:, t, d_cols],
-                        scalar=neg_col[:, t : t + 1],
-                        in1=acc[t][h][:],
+                        out=res[:],
+                        in0=t_sb[blk][:, t, d_cols],
+                        scalar=neg_col[blk][:, t : t + 1],
+                        in1=acc[blk, t, h][:],
                         op0=ALU.mult,
                         op1=ALU.add,
                     )
-                store_queue.dma_start(out=out[n0 + t * P : n0 + (t + 1) * P, :], in_=res[:])
+                    nc.sync.dma_start(out=out[n_rows, d_cols], in_=res[:])
+
+        for i in range(LOAD_AHEAD):
+            load_chunk(i)
+            if AHEAD <= i < AHEAD + X_BUFS:
+                load_x(i - AHEAD)
+        for i in range(AHEAD):
+            mask_and_exp(i)
+
+        for k in range(CHUNKS + 2):
+            closing = k > PASSES and k % PASSES == 1
+            if k + LOAD_AHEAD < CHUNKS:
+                load_chunk(k + LOAD_AHEAD)
+            if k < CHUNKS and k % PASSES == 1:
+                load_patterns(k // PASSES)
+            if k < CHUNKS:
+                product(k)
+            if closing:
+                sum_columns(k // PASSES - 1)
+            if k + AHEAD < CHUNKS:
+                mask_and_exp(k + AHEAD)
+            if k < PASSES:
+                regroup_x(k)
+                if k + X_BUFS < PASSES:
+                    load_x(k + X_BUFS)
+            if closing:
+                finish_block(k // PASSES - 1)
+            if 1 <= k <= PASSES:
+                quantise_x(k - 1)
+            if 1 <= k <= CHUNKS:
+                quantise_and_multiply(k - 1)

@@ -1,6 +1,7 @@
 from contextlib import ExitStack
 
 import concourse.mybir as mybir
+from concourse.masks import make_identity
 
 F32 = mybir.dt.float32
 BF16 = mybir.dt.bfloat16
@@ -10,6 +11,7 @@ E4M3X4 = mybir.dt.float8_e4m3fn_x4
 E5M2X4 = mybir.dt.float8_e5m2_x4
 ALU = mybir.AluOpType
 EXP = mybir.ActivationFunctionType.Exp
+COPY = mybir.ActivationFunctionType.Copy
 
 TOKENS, PATTERNS, FEATURES = 2560, 1536, 1024
 FLOPS = 2 * TOKENS * PATTERNS * FEATURES
@@ -25,7 +27,6 @@ CHUNKS = BLOCKS * PASSES
 HALF = 512
 HALVES = FEATURES // HALF
 RUN = 4
-COL_COPIES = 32
 AHEAD = 2
 LOAD_BUFS = 5
 LOAD_AHEAD = LOAD_BUFS + AHEAD - 1
@@ -53,8 +54,8 @@ def tile_patternlayer_v_kernel(tc, inputs, train_data, dist, grad_out, out):
         col_pool = ctx.enter_context(tc.psum_pool(name="col_pool", bufs=2))
         ctx.enter_context(tc.manual_schedule())
 
-        neg_ones = keep.tile([P, COL_COPIES], F32)
-        nc.vector.memset(neg_ones[:], -1.0)
+        identity = keep.tile([P, P], F32)
+        make_identity(nc, identity[:])
         x_codes = keep.tile([P, PASSES, FEATURES], U32, align_bytes=64)
         x_scales = keep.tile([P, PASSES, FEATURES], U8, align_bytes=64)
 
@@ -118,14 +119,14 @@ def tile_patternlayer_v_kernel(tc, inputs, train_data, dist, grad_out, out):
             if c == 0:
                 col_ps[blk] = col_pool.tile([P, HALF], F32, name="col_ps")
             for t in range(N_TILES):
-                first = (t * PASSES + c) * COL_COPIES
                 for j in range(PACK):
                     nc.tensor.matmul(
-                        out=col_ps[blk][:, first : first + COL_COPIES],
+                        out=col_ps[blk][:, t * P : (t + 1) * P],
                         lhsT=e32[i][:, j, t * P : (t + 1) * P],
-                        rhs=neg_ones[:],
-                        start=(j == 0),
-                        stop=(j == PACK - 1),
+                        rhs=identity[:],
+                        is_transpose=True,
+                        start=(c == 0 and t == 0 and j == 0),
+                        stop=(c == PASSES - 1 and t == N_TILES - 1 and j == PACK - 1),
                     )
             e16[i] = work.tile([P, BLOCK, PACK], BF16, name="e16", align_bytes=64)
             for t in range(N_TILES):
@@ -163,14 +164,15 @@ def tile_patternlayer_v_kernel(tc, inputs, train_data, dist, grad_out, out):
 
         def sum_columns(blk):
             neg_col[blk] = results.tile([P, N_TILES], F32, name="neg_col", bufs=2)
-            nc.vector.tensor_reduce(
-                out=neg_col[blk][:],
-                in_=col_ps[blk][:, 0 : N_TILES * PASSES * COL_COPIES].rearrange(
-                    "p (t c k) -> p t c k", t=N_TILES, c=PASSES
-                )[:, :, :, 0],
-                axis=mybir.AxisListType.X,
-                op=ALU.add,
-            )
+            unread = results.tile([P, N_TILES, P], BF16, bufs=2)
+            for t in range(N_TILES):
+                nc.scalar.activation(
+                    out=unread[:, t, :],
+                    in_=col_ps[blk][:, t * P : (t + 1) * P],
+                    func=COPY,
+                    scale=-1.0,
+                    accum_out=neg_col[blk][:, t : t + 1],
+                )
 
         def finish_block(blk):
             for t in range(N_TILES):
@@ -192,8 +194,8 @@ def tile_patternlayer_v_kernel(tc, inputs, train_data, dist, grad_out, out):
             load_chunk(i)
             if AHEAD <= i < AHEAD + X_BUFS:
                 load_x(i - AHEAD)
-        for i in range(AHEAD):
-            mask_and_exp(i)
+        mask_and_exp(0)
+        masked = 1
 
         for k in range(CHUNKS + 2):
             closing = k > PASSES and k % PASSES == 1
@@ -205,8 +207,9 @@ def tile_patternlayer_v_kernel(tc, inputs, train_data, dist, grad_out, out):
                 product(k)
             if closing:
                 sum_columns(k // PASSES - 1)
-            if k + AHEAD < CHUNKS:
-                mask_and_exp(k + AHEAD)
+            for i in range(masked, min(k + AHEAD, CHUNKS - 1) + 1):
+                mask_and_exp(i)
+            masked = max(masked, min(k + AHEAD, CHUNKS - 1) + 1)
             if k < PASSES:
                 regroup_x(k)
                 if k + X_BUFS < PASSES:

@@ -30,7 +30,7 @@ RUN = 4
 AHEAD = 2
 LOAD_BUFS = 5
 LOAD_AHEAD = LOAD_BUFS + AHEAD - 1
-X_BUFS = 3
+PATTERNS_STEP = 3
 
 
 def regroup(copy, grouped, rows):
@@ -47,7 +47,7 @@ def tile_patternlayer_v_kernel(tc, inputs, train_data, dist, grad_out, out):
         loads = ctx.enter_context(tc.tile_pool(name="loads", bufs=LOAD_BUFS))
         work = ctx.enter_context(tc.tile_pool(name="work", bufs=3))
         coded = ctx.enter_context(tc.tile_pool(name="coded", bufs=4))
-        x_stage = ctx.enter_context(tc.tile_pool(name="x_stage", bufs=X_BUFS))
+        x_stage = ctx.enter_context(tc.tile_pool(name="x_stage", bufs=PASSES))
         t_pool = ctx.enter_context(tc.tile_pool(name="t_pool", bufs=2))
         results = ctx.enter_context(tc.tile_pool(name="results", bufs=6))
         acc_pool = ctx.enter_context(tc.psum_pool(name="acc_pool", bufs=N_TILES * HALVES))
@@ -70,6 +70,8 @@ def tile_patternlayer_v_kernel(tc, inputs, train_data, dist, grad_out, out):
             nc.sync.dma_start(out=r[i][:], in_=dist[rows, cols].rearrange("(p j) n -> p j n", j=PACK))
             g[i] = loads.tile([P, PACK, BLOCK], BF16, name="g")
             nc.sync.dma_start(out=g[i][:], in_=grad_out[rows, cols].rearrange("(p j) n -> p j n", j=PACK))
+            if 0 <= i - AHEAD < PASSES:
+                load_x(i - AHEAD)
 
         def load_x(c):
             x_raw[c] = x_stage.tile([P, PACK, FEATURES], BF16, name="x_raw")
@@ -192,8 +194,6 @@ def tile_patternlayer_v_kernel(tc, inputs, train_data, dist, grad_out, out):
 
         for i in range(LOAD_AHEAD):
             load_chunk(i)
-            if AHEAD <= i < AHEAD + X_BUFS:
-                load_x(i - AHEAD)
         mask_and_exp(0)
         masked = 1
 
@@ -201,19 +201,17 @@ def tile_patternlayer_v_kernel(tc, inputs, train_data, dist, grad_out, out):
             closing = k > PASSES and k % PASSES == 1
             if k + LOAD_AHEAD < CHUNKS:
                 load_chunk(k + LOAD_AHEAD)
-            if k < CHUNKS and k % PASSES == 1:
+            if k < CHUNKS and k % PASSES == PATTERNS_STEP:
                 load_patterns(k // PASSES)
             if k < CHUNKS:
                 product(k)
-            if closing:
+            if k >= PASSES and k % PASSES == 0:
                 sum_columns(k // PASSES - 1)
             for i in range(masked, min(k + AHEAD, CHUNKS - 1) + 1):
                 mask_and_exp(i)
             masked = max(masked, min(k + AHEAD, CHUNKS - 1) + 1)
             if k < PASSES:
                 regroup_x(k)
-                if k + X_BUFS < PASSES:
-                    load_x(k + X_BUFS)
             if closing:
                 finish_block(k // PASSES - 1)
             if 1 <= k <= PASSES:

@@ -20,7 +20,7 @@ P = 128
 PACK = 4
 K_PASS = P * PACK
 PASSES = TOKENS // K_PASS
-BLOCK = 384
+BLOCK = 512
 N_TILES = BLOCK // P
 BLOCKS = PATTERNS // BLOCK
 CHUNKS = BLOCKS * PASSES
@@ -28,9 +28,11 @@ HALF = 512
 HALVES = FEATURES // HALF
 RUN = 4
 AHEAD = 2
-LOAD_BUFS = 5
+LOAD_BUFS = 4
 LOAD_AHEAD = LOAD_BUFS + AHEAD - 1
 PATTERNS_STEP = 3
+OPEN = N_TILES * HALVES - 1
+COPY_COLS = 256
 
 
 def regroup(copy, grouped, rows):
@@ -46,12 +48,12 @@ def tile_patternlayer_v_kernel(tc, inputs, train_data, dist, grad_out, out):
         keep = ctx.enter_context(tc.tile_pool(name="keep", bufs=1))
         loads = ctx.enter_context(tc.tile_pool(name="loads", bufs=LOAD_BUFS))
         work = ctx.enter_context(tc.tile_pool(name="work", bufs=3))
-        coded = ctx.enter_context(tc.tile_pool(name="coded", bufs=4))
-        x_stage = ctx.enter_context(tc.tile_pool(name="x_stage", bufs=PASSES))
+        coded = ctx.enter_context(tc.tile_pool(name="coded", bufs=PASSES + 1))
+        x_stage = ctx.enter_context(tc.tile_pool(name="x_stage", bufs=PASSES - 1))
         t_pool = ctx.enter_context(tc.tile_pool(name="t_pool", bufs=2))
-        results = ctx.enter_context(tc.tile_pool(name="results", bufs=6))
-        acc_pool = ctx.enter_context(tc.psum_pool(name="acc_pool", bufs=N_TILES * HALVES))
-        col_pool = ctx.enter_context(tc.psum_pool(name="col_pool", bufs=2))
+        results = ctx.enter_context(tc.tile_pool(name="results", bufs=8))
+        acc_pool = ctx.enter_context(tc.psum_pool(name="acc_pool", bufs=OPEN))
+        col_pool = ctx.enter_context(tc.psum_pool(name="col_pool", bufs=1))
         ctx.enter_context(tc.manual_schedule())
 
         identity = keep.tile([P, P], F32)
@@ -61,15 +63,20 @@ def tile_patternlayer_v_kernel(tc, inputs, train_data, dist, grad_out, out):
 
         r, g, prob, g_kept, e32, e16 = {}, {}, {}, {}, {}, {}
         x_raw, x_grp, t_sb, col_ps, neg_col, acc = {}, {}, {}, {}, {}, {}
+        e_codes, e_scales = {}, {}
+
+        def pieces(i):
+            return [slice(j, j + 1) for j in range(PACK)] if i == 0 else [slice(0, PACK)]
 
         def load_chunk(i):
             blk, c = divmod(i, PASSES)
             rows = slice(c * K_PASS, (c + 1) * K_PASS)
             cols = slice(blk * BLOCK, (blk + 1) * BLOCK)
             r[i] = loads.tile([P, PACK, BLOCK], F32, name="r")
-            nc.sync.dma_start(out=r[i][:], in_=dist[rows, cols].rearrange("(p j) n -> p j n", j=PACK))
             g[i] = loads.tile([P, PACK, BLOCK], BF16, name="g")
-            nc.sync.dma_start(out=g[i][:], in_=grad_out[rows, cols].rearrange("(p j) n -> p j n", j=PACK))
+            for js in pieces(i):
+                nc.sync.dma_start(out=r[i][:, js, :], in_=dist[rows, cols].rearrange("(p j) n -> p j n", j=PACK)[:, js, :])
+                nc.sync.dma_start(out=g[i][:, js, :], in_=grad_out[rows, cols].rearrange("(p j) n -> p j n", j=PACK)[:, js, :])
             if 0 <= i - AHEAD < PASSES:
                 load_x(i - AHEAD)
 
@@ -88,11 +95,12 @@ def tile_patternlayer_v_kernel(tc, inputs, train_data, dist, grad_out, out):
 
         def mask_and_exp(i):
             g_kept[i] = work.tile([P, PACK, BLOCK], BF16, name="g_kept")
-            nc.vector.scalar_tensor_tensor(
-                out=g_kept[i][:], in0=r[i][:], scalar=0.0, in1=g[i][:], op0=ALU.is_gt, op1=ALU.mult
-            )
             prob[i] = work.tile([P, PACK, BLOCK], F32, name="prob")
-            nc.scalar.activation(out=prob[i][:], in_=r[i][:], func=EXP, scale=-0.5)
+            for js in pieces(i):
+                nc.vector.scalar_tensor_tensor(
+                    out=g_kept[i][:, js, :], in0=r[i][:, js, :], scalar=0.0, in1=g[i][:, js, :], op0=ALU.is_gt, op1=ALU.mult
+                )
+                nc.scalar.activation(out=prob[i][:, js, :], in_=r[i][:, js, :], func=EXP, scale=-0.5)
 
         def regroup_x(c):
             for h in range(HALVES):
@@ -114,7 +122,7 @@ def tile_patternlayer_v_kernel(tc, inputs, train_data, dist, grad_out, out):
 
         def product(i):
             blk, c = divmod(i, PASSES)
-            e32[i] = work.tile([P, PACK, BLOCK], F32, name="e32")
+            e32[i] = work.tile([P, PACK, BLOCK], F32, name="e32", bufs=2)
             nc.vector.scalar_tensor_tensor(
                 out=e32[i][:], in0=prob[i][:], scalar=1.0, in1=g_kept[i][:], op0=ALU.min, op1=ALU.mult
             )
@@ -130,39 +138,39 @@ def tile_patternlayer_v_kernel(tc, inputs, train_data, dist, grad_out, out):
                         start=(c == 0 and t == 0 and j == 0),
                         stop=(c == PASSES - 1 and t == N_TILES - 1 and j == PACK - 1),
                     )
-            e16[i] = work.tile([P, BLOCK, PACK], BF16, name="e16", align_bytes=64)
-            for t in range(N_TILES):
-                n_cols = slice(t * P, (t + 1) * P)
+            e16[i] = work.tile([P, BLOCK, PACK], BF16, name="e16", align_bytes=64, bufs=2)
+            for n0 in range(0, BLOCK, COPY_COLS):
+                n_cols = slice(n0, n0 + COPY_COLS)
                 regroup(nc.scalar.copy, e16[i][:, n_cols, :], e32[i][:, :, n_cols])
+
+        def multiply(blk, c, t, h):
+            n_cols = slice(t * P, (t + 1) * P)
+            d_cols = slice(h * HALF, (h + 1) * HALF)
+            nc.tensor.matmul_mx(
+                out=acc[blk, t, h][:],
+                lhsT=e_codes[blk, c][:, n_cols].bitcast(E5M2X4),
+                lhsT_scale=e_scales[blk, c][:, n_cols],
+                rhs=x_codes[:, c, d_cols].bitcast(E4M3X4),
+                rhs_scale=x_scales[:, c, d_cols],
+                start=(c == 0),
+                stop=(c == PASSES - 1),
+            )
 
         def quantise_and_multiply(i):
             blk, c = divmod(i, PASSES)
+            sums = [(t, h) for t in range(N_TILES) for h in range(HALVES)][:OPEN]
             if c == 0:
-                for t in range(N_TILES):
-                    for h in range(HALVES):
-                        acc[blk, t, h] = acc_pool.tile([P, HALF], F32, name="acc")
-            e_codes = coded.tile([P, BLOCK], U32, align_bytes=64)
-            e_scales = coded.tile([P, BLOCK], U8, align_bytes=64)
-            for t in range(N_TILES):
-                n_cols = slice(t * P, (t + 1) * P)
-                nc.vector.quantize_mx(
-                    out=e_codes[:, n_cols].bitcast(E5M2X4),
-                    scales=e_scales[:, n_cols],
-                    in_=e16[i][:, n_cols, :].rearrange("p n j -> p (n j)"),
-                )
-            for t in range(N_TILES):
-                n_cols = slice(t * P, (t + 1) * P)
-                for h in range(HALVES):
-                    d_cols = slice(h * HALF, (h + 1) * HALF)
-                    nc.tensor.matmul_mx(
-                        out=acc[blk, t, h][:],
-                        lhsT=e_codes[:, n_cols].bitcast(E5M2X4),
-                        lhsT_scale=e_scales[:, n_cols],
-                        rhs=x_codes[:, c, d_cols].bitcast(E4M3X4),
-                        rhs_scale=x_scales[:, c, d_cols],
-                        start=(c == 0),
-                        stop=(c == PASSES - 1),
-                    )
+                for t, h in sums:
+                    acc[blk, t, h] = acc_pool.tile([P, HALF], F32, name="acc")
+            e_codes[blk, c] = coded.tile([P, BLOCK], U32, name="e_codes", align_bytes=64)
+            e_scales[blk, c] = coded.tile([P, BLOCK], U8, name="e_scales", align_bytes=64)
+            nc.vector.quantize_mx(
+                out=e_codes[blk, c][:].bitcast(E5M2X4),
+                scales=e_scales[blk, c][:],
+                in_=e16[i][:].rearrange("p n j -> p (n j)"),
+            )
+            for t, h in sums:
+                multiply(blk, c, t, h)
 
         def sum_columns(blk):
             neg_col[blk] = results.tile([P, N_TILES], F32, name="neg_col", bufs=2)
@@ -191,6 +199,10 @@ def tile_patternlayer_v_kernel(tc, inputs, train_data, dist, grad_out, out):
                         op1=ALU.add,
                     )
                     nc.sync.dma_start(out=out[n_rows, d_cols], in_=res[:])
+                    if (t, h) == (0, 0):
+                        acc[blk, N_TILES - 1, HALVES - 1] = acc_pool.tile([P, HALF], F32, name="acc")
+                        for c in range(PASSES):
+                            multiply(blk, c, N_TILES - 1, HALVES - 1)
 
         for i in range(LOAD_AHEAD):
             load_chunk(i)
@@ -203,10 +215,10 @@ def tile_patternlayer_v_kernel(tc, inputs, train_data, dist, grad_out, out):
                 load_chunk(k + LOAD_AHEAD)
             if k < CHUNKS and k % PASSES == PATTERNS_STEP:
                 load_patterns(k // PASSES)
-            if k < CHUNKS:
-                product(k)
             if k >= PASSES and k % PASSES == 0:
                 sum_columns(k // PASSES - 1)
+            if k < CHUNKS:
+                product(k)
             for i in range(masked, min(k + AHEAD, CHUNKS - 1) + 1):
                 mask_and_exp(i)
             masked = max(masked, min(k + AHEAD, CHUNKS - 1) + 1)

@@ -20,19 +20,18 @@ P = 128
 PACK = 4
 K_PASS = P * PACK
 PASSES = TOKENS // K_PASS
-BLOCK = 512
-N_TILES = BLOCK // P
-BLOCKS = PATTERNS // BLOCK
-CHUNKS = BLOCKS * PASSES
+WIDTHS = (512, 512, 384, 128)
+STARTS = (0, 512, 1024, 1408)
+LAST = len(WIDTHS) * PASSES - 1
 HALF = 512
 HALVES = FEATURES // HALF
 RUN = 4
-AHEAD = 2
-LOAD_BUFS = 4
-LOAD_AHEAD = LOAD_BUFS + AHEAD - 1
-PATTERNS_STEP = 3
-OPEN = N_TILES * HALVES - 1
-COPY_COLS = 256
+LOAD_BUFS = 5
+LOAD_AHEAD = LOAD_BUFS
+HEAD_CHUNKS = 2
+PATTERNS_PASS = 3
+BANKS = 7
+PART = 256
 
 
 def regroup(copy, grouped, rows):
@@ -47,12 +46,12 @@ def tile_patternlayer_v_kernel(tc, inputs, train_data, dist, grad_out, out):
     with ExitStack() as ctx:
         keep = ctx.enter_context(tc.tile_pool(name="keep", bufs=1))
         loads = ctx.enter_context(tc.tile_pool(name="loads", bufs=LOAD_BUFS))
-        work = ctx.enter_context(tc.tile_pool(name="work", bufs=3))
+        work = ctx.enter_context(tc.tile_pool(name="work", bufs=2))
         coded = ctx.enter_context(tc.tile_pool(name="coded", bufs=PASSES + 1))
-        x_stage = ctx.enter_context(tc.tile_pool(name="x_stage", bufs=PASSES - 1))
+        x_stage = ctx.enter_context(tc.tile_pool(name="x_stage", bufs=PASSES))
         t_pool = ctx.enter_context(tc.tile_pool(name="t_pool", bufs=2))
         results = ctx.enter_context(tc.tile_pool(name="results", bufs=8))
-        acc_pool = ctx.enter_context(tc.psum_pool(name="acc_pool", bufs=OPEN))
+        acc_pool = ctx.enter_context(tc.psum_pool(name="acc_pool", bufs=BANKS))
         col_pool = ctx.enter_context(tc.psum_pool(name="col_pool", bufs=1))
         ctx.enter_context(tc.manual_schedule())
 
@@ -64,169 +63,205 @@ def tile_patternlayer_v_kernel(tc, inputs, train_data, dist, grad_out, out):
         r, g, prob, g_kept, e32, e16 = {}, {}, {}, {}, {}, {}
         x_raw, x_grp, t_sb, col_ps, neg_col, acc = {}, {}, {}, {}, {}, {}
         e_codes, e_scales = {}, {}
+        halves = [slice(h * HALF, (h + 1) * HALF) for h in range(HALVES)]
+        chunks = [(blk, c) for blk in range(len(WIDTHS)) for c in range(PASSES)]
 
-        def pieces(i):
-            return [slice(j, j + 1) for j in range(PACK)] if i == 0 else [slice(0, PACK)]
+        def tile_cols(t):
+            return slice(t * P, (t + 1) * P)
+
+        def sums_of(blk):
+            return [(t, h) for t in range(WIDTHS[blk] // P) for h in range(HALVES)]
+
+        def parts(blk):
+            return [slice(n0, min(n0 + PART, WIDTHS[blk])) for n0 in range(0, WIDTHS[blk], PART)]
+
+        def slots(i):
+            return [slice(j, j + 1) for j in range(PACK)] if i < HEAD_CHUNKS else [slice(0, PACK)]
 
         def load_chunk(i):
-            blk, c = divmod(i, PASSES)
+            blk, c = chunks[i]
             rows = slice(c * K_PASS, (c + 1) * K_PASS)
-            cols = slice(blk * BLOCK, (blk + 1) * BLOCK)
-            r[i] = loads.tile([P, PACK, BLOCK], F32, name="r")
-            g[i] = loads.tile([P, PACK, BLOCK], BF16, name="g")
-            for js in pieces(i):
+            cols = slice(STARTS[blk], STARTS[blk] + WIDTHS[blk])
+            r[i] = loads.tile([P, PACK, WIDTHS[blk]], F32, name="r")
+            g[i] = loads.tile([P, PACK, WIDTHS[blk]], BF16, name="g")
+            for js in slots(i):
                 nc.sync.dma_start(out=r[i][:, js, :], in_=dist[rows, cols].rearrange("(p j) n -> p j n", j=PACK)[:, js, :])
                 nc.sync.dma_start(out=g[i][:, js, :], in_=grad_out[rows, cols].rearrange("(p j) n -> p j n", j=PACK)[:, js, :])
-            if 0 <= i - AHEAD < PASSES:
-                load_x(i - AHEAD)
+            if i < PASSES:
+                load_x(i, 1)
+            if 1 <= i <= PASSES:
+                load_x(i - 1, 0)
 
-        def load_x(c):
-            x_raw[c] = x_stage.tile([P, PACK, FEATURES], BF16, name="x_raw")
+        def load_x(c, h):
+            x_raw[c, h] = x_stage.tile([P, PACK, HALF], BF16, name="x_raw", bufs=PASSES * HALVES)
             nc.sync.dma_start(
-                out=x_raw[c][:], in_=inputs[c * K_PASS : (c + 1) * K_PASS, :].rearrange("(p j) d -> p j d", j=PACK)
+                out=x_raw[c, h][:],
+                in_=inputs[c * K_PASS : (c + 1) * K_PASS, halves[h]].rearrange("(p j) d -> p j d", j=PACK),
             )
 
         def load_patterns(blk):
-            t_sb[blk] = t_pool.tile([P, N_TILES, FEATURES], BF16, name="t_sb")
+            t_sb[blk] = t_pool.tile([P, WIDTHS[blk] // P, FEATURES], BF16, name="t_sb")
             nc.sync.dma_start(
                 out=t_sb[blk][:],
-                in_=train_data[blk * BLOCK : (blk + 1) * BLOCK, :].rearrange("(t p) d -> p t d", p=P),
+                in_=train_data[STARTS[blk] : STARTS[blk] + WIDTHS[blk], :].rearrange("(t p) d -> p t d", p=P),
             )
 
-        def mask_and_exp(i):
-            g_kept[i] = work.tile([P, PACK, BLOCK], BF16, name="g_kept")
-            prob[i] = work.tile([P, PACK, BLOCK], F32, name="prob")
-            for js in pieces(i):
-                nc.vector.scalar_tensor_tensor(
-                    out=g_kept[i][:, js, :], in0=r[i][:, js, :], scalar=0.0, in1=g[i][:, js, :], op0=ALU.is_gt, op1=ALU.mult
-                )
-                nc.scalar.activation(out=prob[i][:, js, :], in_=r[i][:, js, :], func=EXP, scale=-0.5)
+        def exponential(i, js):
+            if i not in prob:
+                prob[i] = work.tile([P, PACK, WIDTHS[chunks[i][0]]], F32, name="prob")
+            nc.scalar.activation(out=prob[i][:, js, :], in_=r[i][:, js, :], func=EXP, scale=-0.5)
 
-        def regroup_x(c):
-            for h in range(HALVES):
-                x_grp[c, h] = x_stage.tile([P, HALF, PACK], BF16, name="x_grp", align_bytes=64, bufs=2 * HALVES)
-                regroup(
-                    nc.scalar.copy if h == 0 else nc.vector.tensor_copy,
-                    x_grp[c, h][:],
-                    x_raw[c][:, :, h * HALF : (h + 1) * HALF],
-                )
-
-        def quantise_x(c):
-            for h in range(HALVES):
-                d_cols = slice(h * HALF, (h + 1) * HALF)
-                nc.vector.quantize_mx(
-                    out=x_codes[:, c, d_cols].bitcast(E4M3X4),
-                    scales=x_scales[:, c, d_cols],
-                    in_=x_grp[c, h][:].rearrange("p d j -> p (d j)"),
-                )
-
-        def product(i):
-            blk, c = divmod(i, PASSES)
-            e32[i] = work.tile([P, PACK, BLOCK], F32, name="e32", bufs=2)
+        def mask(i, js):
+            if i not in g_kept:
+                g_kept[i] = work.tile([P, PACK, WIDTHS[chunks[i][0]]], BF16, name="g_kept", bufs=3)
             nc.vector.scalar_tensor_tensor(
-                out=e32[i][:], in0=prob[i][:], scalar=1.0, in1=g_kept[i][:], op0=ALU.min, op1=ALU.mult
+                out=g_kept[i][:, js, :], in0=r[i][:, js, :], scalar=0.0, in1=g[i][:, js, :], op0=ALU.is_gt, op1=ALU.mult
             )
+
+        def times(i, js):
+            if i not in e32:
+                e32[i] = work.tile([P, PACK, WIDTHS[chunks[i][0]]], F32, name="e32")
+            nc.vector.scalar_tensor_tensor(
+                out=e32[i][:, js, :], in0=prob[i][:, js, :], scalar=1.0, in1=g_kept[i][:, js, :], op0=ALU.min, op1=ALU.mult
+            )
+
+        def add_columns_and_regroup(i):
+            blk, c = chunks[i]
+            n_tiles = WIDTHS[blk] // P
             if c == 0:
                 col_ps[blk] = col_pool.tile([P, HALF], F32, name="col_ps")
-            for t in range(N_TILES):
+            for t in range(n_tiles):
                 for j in range(PACK):
                     nc.tensor.matmul(
-                        out=col_ps[blk][:, t * P : (t + 1) * P],
-                        lhsT=e32[i][:, j, t * P : (t + 1) * P],
+                        out=col_ps[blk][:, tile_cols(t)],
+                        lhsT=e32[i][:, j, tile_cols(t)],
                         rhs=identity[:],
                         is_transpose=True,
                         start=(c == 0 and t == 0 and j == 0),
-                        stop=(c == PASSES - 1 and t == N_TILES - 1 and j == PACK - 1),
+                        stop=(c == PASSES - 1 and t == n_tiles - 1 and j == PACK - 1),
                     )
-            e16[i] = work.tile([P, BLOCK, PACK], BF16, name="e16", align_bytes=64, bufs=2)
-            for n0 in range(0, BLOCK, COPY_COLS):
-                n_cols = slice(n0, n0 + COPY_COLS)
+            e16[i] = work.tile([P, WIDTHS[blk], PACK], BF16, name="e16", align_bytes=64)
+            for n_cols in parts(blk):
                 regroup(nc.scalar.copy, e16[i][:, n_cols, :], e32[i][:, :, n_cols])
 
+        def regroup_x(c):
+            for h in range(HALVES):
+                x_grp[c, h] = x_stage.tile([P, HALF, PACK], BF16, name="x_grp", align_bytes=64, bufs=HALVES)
+                regroup(nc.scalar.copy if h == 0 else nc.vector.tensor_copy, x_grp[c, h][:], x_raw[c, h][:])
+
+        def quantise_x(c, h):
+            nc.vector.quantize_mx(
+                out=x_codes[:, c, halves[h]].bitcast(E4M3X4),
+                scales=x_scales[:, c, halves[h]],
+                in_=x_grp[c, h][:].rearrange("p d j -> p (d j)"),
+            )
+
         def multiply(blk, c, t, h):
-            n_cols = slice(t * P, (t + 1) * P)
-            d_cols = slice(h * HALF, (h + 1) * HALF)
             nc.tensor.matmul_mx(
                 out=acc[blk, t, h][:],
-                lhsT=e_codes[blk, c][:, n_cols].bitcast(E5M2X4),
-                lhsT_scale=e_scales[blk, c][:, n_cols],
-                rhs=x_codes[:, c, d_cols].bitcast(E4M3X4),
-                rhs_scale=x_scales[:, c, d_cols],
+                lhsT=e_codes[blk, c][:, tile_cols(t)].bitcast(E5M2X4),
+                lhsT_scale=e_scales[blk, c][:, tile_cols(t)],
+                rhs=x_codes[:, c, halves[h]].bitcast(E4M3X4),
+                rhs_scale=x_scales[:, c, halves[h]],
                 start=(c == 0),
                 stop=(c == PASSES - 1),
             )
 
-        def quantise_and_multiply(i):
-            blk, c = divmod(i, PASSES)
-            sums = [(t, h) for t in range(N_TILES) for h in range(HALVES)][:OPEN]
+        def quantise_e(i):
+            blk, c = chunks[i]
+            e_codes[blk, c] = coded.tile([P, WIDTHS[blk]], U32, name="e_codes", align_bytes=64)
+            e_scales[blk, c] = coded.tile([P, WIDTHS[blk]], U8, name="e_scales", align_bytes=64)
+            for n_cols in parts(blk):
+                nc.vector.quantize_mx(
+                    out=e_codes[blk, c][:, n_cols].bitcast(E5M2X4),
+                    scales=e_scales[blk, c][:, n_cols],
+                    in_=e16[i][:, n_cols, :].rearrange("p n j -> p (n j)"),
+                )
+
+        def multiply_chunk(i):
+            blk, c = chunks[i]
             if c == 0:
-                for t, h in sums:
+                for t, h in sums_of(blk)[:BANKS]:
                     acc[blk, t, h] = acc_pool.tile([P, HALF], F32, name="acc")
-            e_codes[blk, c] = coded.tile([P, BLOCK], U32, name="e_codes", align_bytes=64)
-            e_scales[blk, c] = coded.tile([P, BLOCK], U8, name="e_scales", align_bytes=64)
-            nc.vector.quantize_mx(
-                out=e_codes[blk, c][:].bitcast(E5M2X4),
-                scales=e_scales[blk, c][:],
-                in_=e16[i][:].rearrange("p n j -> p (n j)"),
-            )
-            for t, h in sums:
+            for t, h in sums_of(blk)[:BANKS]:
                 multiply(blk, c, t, h)
 
         def sum_columns(blk):
-            neg_col[blk] = results.tile([P, N_TILES], F32, name="neg_col", bufs=2)
-            unread = results.tile([P, N_TILES, P], BF16, bufs=2)
-            for t in range(N_TILES):
+            n_tiles = WIDTHS[blk] // P
+            neg_col[blk] = results.tile([P, n_tiles], F32, name="neg_col", bufs=2)
+            unread = results.tile([P, n_tiles, P], BF16, bufs=2)
+            for t in range(n_tiles):
                 nc.scalar.activation(
                     out=unread[:, t, :],
-                    in_=col_ps[blk][:, t * P : (t + 1) * P],
+                    in_=col_ps[blk][:, tile_cols(t)],
                     func=COPY,
                     scale=-1.0,
                     accum_out=neg_col[blk][:, t : t + 1],
                 )
 
-        def finish_block(blk):
-            for t in range(N_TILES):
-                n_rows = slice(blk * BLOCK + t * P, blk * BLOCK + (t + 1) * P)
-                for h in range(HALVES):
-                    d_cols = slice(h * HALF, (h + 1) * HALF)
-                    res = results.tile([P, HALF], F32)
-                    nc.vector.scalar_tensor_tensor(
-                        out=res[:],
-                        in0=t_sb[blk][:, t, d_cols],
-                        scalar=neg_col[blk][:, t : t + 1],
-                        in1=acc[blk, t, h][:],
-                        op0=ALU.mult,
-                        op1=ALU.add,
-                    )
-                    nc.sync.dma_start(out=out[n_rows, d_cols], in_=res[:])
-                    if (t, h) == (0, 0):
-                        acc[blk, N_TILES - 1, HALVES - 1] = acc_pool.tile([P, HALF], F32, name="acc")
-                        for c in range(PASSES):
-                            multiply(blk, c, N_TILES - 1, HALVES - 1)
+        def finish(blk, t, h):
+            res = results.tile([P, HALF], F32)
+            nc.vector.scalar_tensor_tensor(
+                out=res[:],
+                in0=t_sb[blk][:, t, halves[h]],
+                scalar=neg_col[blk][:, t : t + 1],
+                in1=acc[blk, t, h][:],
+                op0=ALU.mult,
+                op1=ALU.add,
+            )
+            nc.sync.dma_start(out=out[STARTS[blk] + t * P : STARTS[blk] + (t + 1) * P, halves[h]], in_=res[:])
+            if (t, h) == (0, 0):
+                for t_late, h_late in sums_of(blk)[BANKS:]:
+                    acc[blk, t_late, h_late] = acc_pool.tile([P, HALF], F32, name="acc")
+                    for c in range(PASSES):
+                        multiply(blk, c, t_late, h_late)
 
         for i in range(LOAD_AHEAD):
             load_chunk(i)
-        mask_and_exp(0)
-        masked = 1
+        for j, js in enumerate(slots(0)):
+            exponential(0, js)
+            mask(0, js)
+            if j > 0:
+                times(0, slots(0)[j - 1])
+        times(0, slots(0)[-1])
 
-        for k in range(CHUNKS + 2):
-            closing = k > PASSES and k % PASSES == 1
-            if k + LOAD_AHEAD < CHUNKS:
+        def leaving(k, late):
+            found = []
+            for blk in range(len(WIDTHS)):
+                for t, h in sums_of(blk):
+                    held = blk == len(WIDTHS) - 2 and t > 0
+                    if held == late and k == (LAST + t - 1 if held else PASSES * (blk + 1) + 1):
+                        found.append((blk, t, h))
+            return found
+
+        for k in range(len(chunks) + 2):
+            if k + LOAD_AHEAD <= LAST:
                 load_chunk(k + LOAD_AHEAD)
-            if k < CHUNKS and k % PASSES == PATTERNS_STEP:
-                load_patterns(k // PASSES)
+            if k <= LAST and chunks[k][1] == PATTERNS_PASS:
+                load_patterns(chunks[k][0])
             if k >= PASSES and k % PASSES == 0:
                 sum_columns(k // PASSES - 1)
-            if k < CHUNKS:
-                product(k)
-            for i in range(masked, min(k + AHEAD, CHUNKS - 1) + 1):
-                mask_and_exp(i)
-            masked = max(masked, min(k + AHEAD, CHUNKS - 1) + 1)
+            if k + 1 <= LAST:
+                for js in slots(k + 1):
+                    exponential(k + 1, js)
+            if 1 <= k <= LAST:
+                times(k, slice(0, PACK))
+            if k <= LAST:
+                add_columns_and_regroup(k)
+            for blk, t, h in leaving(k, False):
+                finish(blk, t, h)
+            if 1 <= k <= PASSES:
+                quantise_x(k - 1, 1)
+            if 1 <= k <= LAST + 1:
+                quantise_e(k - 1)
+            if 1 <= k <= PASSES:
+                quantise_x(k - 1, 0)
+            if 1 <= k <= LAST + 1:
+                multiply_chunk(k - 1)
+            for blk, t, h in leaving(k, True):
+                finish(blk, t, h)
+            for i in range(len(g_kept), min(k + (1 if k < PASSES - 1 else 2), LAST) + 1):
+                for js in slots(i):
+                    mask(i, js)
             if k < PASSES:
                 regroup_x(k)
-            if closing:
-                finish_block(k // PASSES - 1)
-            if 1 <= k <= PASSES:
-                quantise_x(k - 1)
-            if 1 <= k <= CHUNKS:
-                quantise_and_multiply(k - 1)

@@ -26,10 +26,10 @@ LAST = len(WIDTHS) * PASSES - 1
 HALF = 512
 HALVES = FEATURES // HALF
 RUN = 4
-LOAD_BUFS = 5
+LOAD_BUFS = 4
 LOAD_AHEAD = LOAD_BUFS
-HEAD_CHUNKS = 2
-PATTERNS_PASS = 3
+HEAD_CHUNKS = 1
+PATTERNS_PASS = 1
 BANKS = 7
 PART = 256
 
@@ -76,7 +76,8 @@ def tile_patternlayer_v_kernel(tc, inputs, train_data, dist, grad_out, out):
             return [slice(n0, min(n0 + PART, WIDTHS[blk])) for n0 in range(0, WIDTHS[blk], PART)]
 
         def slots(i):
-            return [slice(j, j + 1) for j in range(PACK)] if i < HEAD_CHUNKS else [slice(0, PACK)]
+            step = 1 if i < HEAD_CHUNKS else 2 if i <= 2 * PASSES else PACK
+            return [slice(j, j + step) for j in range(0, PACK, step)]
 
         def load_chunk(i):
             blk, c = chunks[i]
@@ -84,20 +85,16 @@ def tile_patternlayer_v_kernel(tc, inputs, train_data, dist, grad_out, out):
             cols = slice(STARTS[blk], STARTS[blk] + WIDTHS[blk])
             r[i] = loads.tile([P, PACK, WIDTHS[blk]], F32, name="r")
             g[i] = loads.tile([P, PACK, WIDTHS[blk]], BF16, name="g")
-            for js in slots(i):
+            for js in slots(i) if i < HEAD_CHUNKS else [slice(0, PACK)]:
                 nc.sync.dma_start(out=r[i][:, js, :], in_=dist[rows, cols].rearrange("(p j) n -> p j n", j=PACK)[:, js, :])
                 nc.sync.dma_start(out=g[i][:, js, :], in_=grad_out[rows, cols].rearrange("(p j) n -> p j n", j=PACK)[:, js, :])
-            if i < PASSES:
-                load_x(i, 1)
-            if 1 <= i <= PASSES:
-                load_x(i - 1, 0)
 
-        def load_x(c, h):
-            x_raw[c, h] = x_stage.tile([P, PACK, HALF], BF16, name="x_raw", bufs=PASSES * HALVES)
-            nc.sync.dma_start(
-                out=x_raw[c, h][:],
-                in_=inputs[c * K_PASS : (c + 1) * K_PASS, halves[h]].rearrange("(p j) d -> p j d", j=PACK),
-            )
+        def load_x(c):
+            rows = inputs[c * K_PASS : (c + 1) * K_PASS, :].rearrange("(p j) d -> p j d", j=PACK)
+            whole = x_stage.tile([P, PACK, FEATURES], BF16, name="x_raw")
+            nc.sync.dma_start(out=whole[:], in_=rows)
+            for h in range(HALVES):
+                x_raw[c, h] = whole[:, :, halves[h]]
 
         def load_patterns(blk):
             t_sb[blk] = t_pool.tile([P, WIDTHS[blk] // P, FEATURES], BF16, name="t_sb")
@@ -125,7 +122,7 @@ def tile_patternlayer_v_kernel(tc, inputs, train_data, dist, grad_out, out):
                 out=e32[i][:, js, :], in0=prob[i][:, js, :], scalar=1.0, in1=g_kept[i][:, js, :], op0=ALU.min, op1=ALU.mult
             )
 
-        def add_columns_and_regroup(i):
+        def add_columns(i):
             blk, c = chunks[i]
             n_tiles = WIDTHS[blk] // P
             if c == 0:
@@ -140,14 +137,17 @@ def tile_patternlayer_v_kernel(tc, inputs, train_data, dist, grad_out, out):
                         start=(c == 0 and t == 0 and j == 0),
                         stop=(c == PASSES - 1 and t == n_tiles - 1 and j == PACK - 1),
                     )
+
+        def round_and_regroup(i):
+            blk = chunks[i][0]
             e16[i] = work.tile([P, WIDTHS[blk], PACK], BF16, name="e16", align_bytes=64)
             for n_cols in parts(blk):
                 regroup(nc.scalar.copy, e16[i][:, n_cols, :], e32[i][:, :, n_cols])
 
         def regroup_x(c):
             for h in range(HALVES):
-                x_grp[c, h] = x_stage.tile([P, HALF, PACK], BF16, name="x_grp", align_bytes=64, bufs=HALVES)
-                regroup(nc.scalar.copy if h == 0 else nc.vector.tensor_copy, x_grp[c, h][:], x_raw[c, h][:])
+                x_grp[c, h] = x_stage.tile([P, HALF, PACK], BF16, name="x_grp", align_bytes=64, bufs=2 * HALVES)
+                regroup(nc.scalar.copy if h == 0 else nc.vector.tensor_copy, x_grp[c, h][:], x_raw[c, h][:, :, :])
 
         def quantise_x(c, h):
             nc.vector.quantize_mx(
@@ -216,7 +216,10 @@ def tile_patternlayer_v_kernel(tc, inputs, train_data, dist, grad_out, out):
                     for c in range(PASSES):
                         multiply(blk, c, t_late, h_late)
 
-        for i in range(LOAD_AHEAD):
+        load_chunk(0)
+        for c in range(PASSES):
+            load_x(c)
+        for i in range(1, LOAD_AHEAD):
             load_chunk(i)
         for j, js in enumerate(slots(0)):
             exponential(0, js)
@@ -224,6 +227,14 @@ def tile_patternlayer_v_kernel(tc, inputs, train_data, dist, grad_out, out):
             if j > 0:
                 times(0, slots(0)[j - 1])
         times(0, slots(0)[-1])
+        add_columns(0)
+        round_and_regroup(0)
+        for c in range(PASSES + 1):
+            if c < PASSES:
+                regroup_x(c)
+            if c > 0:
+                quantise_x(c - 1, 1)
+                quantise_x(c - 1, 0)
 
         def leaving(k, late):
             found = []
@@ -239,29 +250,27 @@ def tile_patternlayer_v_kernel(tc, inputs, train_data, dist, grad_out, out):
                 load_chunk(k + LOAD_AHEAD)
             if k <= LAST and chunks[k][1] == PATTERNS_PASS:
                 load_patterns(chunks[k][0])
-            if k >= PASSES and k % PASSES == 0:
-                sum_columns(k // PASSES - 1)
             if k + 1 <= LAST:
                 for js in slots(k + 1):
                     exponential(k + 1, js)
+            if k >= PASSES and k % PASSES == 0:
+                sum_columns(k // PASSES - 1)
             if 1 <= k <= LAST:
-                times(k, slice(0, PACK))
-            if k <= LAST:
-                add_columns_and_regroup(k)
+                for js in slots(k):
+                    times(k, js)
+            if k <= LAST and k % PASSES > 0:
+                add_columns(k)
+            if 1 <= k <= LAST:
+                round_and_regroup(k)
             for blk, t, h in leaving(k, False):
                 finish(blk, t, h)
-            if 1 <= k <= PASSES:
-                quantise_x(k - 1, 1)
             if 1 <= k <= LAST + 1:
                 quantise_e(k - 1)
-            if 1 <= k <= PASSES:
-                quantise_x(k - 1, 0)
-            if 1 <= k <= LAST + 1:
                 multiply_chunk(k - 1)
+            if 1 <= k <= LAST and k % PASSES == 0:
+                add_columns(k)
             for blk, t, h in leaving(k, True):
                 finish(blk, t, h)
-            for i in range(len(g_kept), min(k + (1 if k < PASSES - 1 else 2), LAST) + 1):
+            for i in range(len(g_kept), min(k + (1 if k < 2 * PASSES else 2), LAST) + 1):
                 for js in slots(i):
                     mask(i, js)
-            if k < PASSES:
-                regroup_x(k)

@@ -258,7 +258,8 @@ def tile_patternlayer_v_kernel(tc, inputs, train_data, dist, grad_out, out):
             if 1 <= k <= LAST:
                 for js in slots(k):
                     times(k, js)
-            if k <= LAST and k % PASSES > 0:
+            passes_first = k <= 2 * PASSES or k % PASSES == 0
+            if k <= LAST and not passes_first:
                 add_columns(k)
             if 1 <= k <= LAST:
                 round_and_regroup(k)
@@ -267,7 +268,7 @@ def tile_patternlayer_v_kernel(tc, inputs, train_data, dist, grad_out, out):
             if 1 <= k <= LAST + 1:
                 quantise_e(k - 1)
                 multiply_chunk(k - 1)
-            if 1 <= k <= LAST and k % PASSES == 0:
+            if 1 <= k <= LAST and passes_first:
                 add_columns(k)
             for blk, t, h in leaving(k, True):
                 finish(blk, t, h)

@@ -50,7 +50,7 @@ def tile_patternlayer_v_kernel(tc, inputs, train_data, dist, grad_out, out):
         coded = ctx.enter_context(tc.tile_pool(name="coded", bufs=PASSES + 1))
         x_stage = ctx.enter_context(tc.tile_pool(name="x_stage", bufs=PASSES))
         t_pool = ctx.enter_context(tc.tile_pool(name="t_pool", bufs=2))
-        results = ctx.enter_context(tc.tile_pool(name="results", bufs=8))
+        results = ctx.enter_context(tc.tile_pool(name="results", bufs=4))
         acc_pool = ctx.enter_context(tc.psum_pool(name="acc_pool", bufs=BANKS))
         col_pool = ctx.enter_context(tc.psum_pool(name="col_pool", bufs=1))
         ctx.enter_context(tc.manual_schedule())
@@ -62,7 +62,7 @@ def tile_patternlayer_v_kernel(tc, inputs, train_data, dist, grad_out, out):
 
         r, g, prob, g_kept, e32, e16 = {}, {}, {}, {}, {}, {}
         x_raw, x_grp, t_sb, col_ps, neg_col, acc = {}, {}, {}, {}, {}, {}
-        e_codes, e_scales = {}, {}
+        e_codes, e_scales, res = {}, {}, {}
         halves = [slice(h * HALF, (h + 1) * HALF) for h in range(HALVES)]
         chunks = [(blk, c) for blk in range(len(WIDTHS)) for c in range(PASSES)]
 
@@ -146,7 +146,9 @@ def tile_patternlayer_v_kernel(tc, inputs, train_data, dist, grad_out, out):
 
         def regroup_x(c):
             for h in range(HALVES):
-                x_grp[c, h] = x_stage.tile([P, HALF, PACK], BF16, name="x_grp", align_bytes=64, bufs=2 * HALVES)
+                x_grp[c, h] = x_stage.tile(
+                    [P, HALF, PACK], BF16, name="x_grp_s" if h == 0 else "x_grp_v", align_bytes=64, bufs=3 if h == 0 else 2
+                )
                 regroup(nc.scalar.copy if h == 0 else nc.vector.tensor_copy, x_grp[c, h][:], x_raw[c, h][:, :, :])
 
         def quantise_x(c, h):
@@ -171,7 +173,7 @@ def tile_patternlayer_v_kernel(tc, inputs, train_data, dist, grad_out, out):
             blk, c = chunks[i]
             e_codes[blk, c] = coded.tile([P, WIDTHS[blk]], U32, name="e_codes", align_bytes=64)
             e_scales[blk, c] = coded.tile([P, WIDTHS[blk]], U8, name="e_scales", align_bytes=64)
-            for n_cols in parts(blk):
+            for n_cols in [slice(0, WIDTHS[blk])] if WIDTHS[blk] in (P, 2 * P, 4 * P) else parts(blk):
                 nc.vector.quantize_mx(
                     out=e_codes[blk, c][:, n_cols].bitcast(E5M2X4),
                     scales=e_scales[blk, c][:, n_cols],
@@ -200,16 +202,21 @@ def tile_patternlayer_v_kernel(tc, inputs, train_data, dist, grad_out, out):
                 )
 
         def finish(blk, t, h):
-            res = results.tile([P, HALF], F32)
+            if h == 0:
+                res[blk, t] = results.tile([P, FEATURES], F32, name="res")
             nc.vector.scalar_tensor_tensor(
-                out=res[:],
+                out=res[blk, t][:, halves[h]],
                 in0=t_sb[blk][:, t, halves[h]],
                 scalar=neg_col[blk][:, t : t + 1],
                 in1=acc[blk, t, h][:],
                 op0=ALU.mult,
                 op1=ALU.add,
             )
-            nc.sync.dma_start(out=out[STARTS[blk] + t * P : STARTS[blk] + (t + 1) * P, halves[h]], in_=res[:])
+            n_rows = slice(STARTS[blk] + t * P, STARTS[blk] + (t + 1) * P)
+            if blk == len(WIDTHS) - 1 and t == WIDTHS[blk] // P - 1:
+                nc.sync.dma_start(out=out[n_rows, halves[h]], in_=res[blk, t][:, halves[h]])
+            elif h == HALVES - 1:
+                nc.sync.dma_start(out=out[n_rows, :], in_=res[blk, t][:])
             if (t, h) == (0, 0):
                 for t_late, h_late in sums_of(blk)[BANKS:]:
                     acc[blk, t_late, h_late] = acc_pool.tile([P, HALF], F32, name="acc")
@@ -232,9 +239,10 @@ def tile_patternlayer_v_kernel(tc, inputs, train_data, dist, grad_out, out):
         for c in range(PASSES + 1):
             if c < PASSES:
                 regroup_x(c)
-            if c > 0:
+            if c >= 1:
                 quantise_x(c - 1, 1)
-                quantise_x(c - 1, 0)
+            if c >= 2:
+                quantise_x(c - 2, 0)
 
         def leaving(k, late):
             found = []
@@ -275,3 +283,5 @@ def tile_patternlayer_v_kernel(tc, inputs, train_data, dist, grad_out, out):
             for i in range(len(g_kept), min(k + (1 if k < 2 * PASSES else 2), LAST) + 1):
                 for js in slots(i):
                     mask(i, js)
+            if k == 0:
+                quantise_x(PASSES - 1, 0)

@@ -28,6 +28,7 @@ HALVES = FEATURES // HALF
 RUN = 4
 LOAD_BUFS = 4
 LOAD_AHEAD = LOAD_BUFS
+HALVED = 5
 HEAD_CHUNKS = 1
 PATTERNS_PASS = 1
 BANKS = 7
@@ -76,7 +77,7 @@ def tile_patternlayer_v_kernel(tc, inputs, train_data, dist, grad_out, out):
             return [slice(n0, min(n0 + PART, WIDTHS[blk])) for n0 in range(0, WIDTHS[blk], PART)]
 
         def slots(i):
-            step = 1 if i < HEAD_CHUNKS else 2 if i <= 2 * PASSES else PACK
+            step = 1 if i < HEAD_CHUNKS else 2 if i <= HALVED else PACK
             return [slice(j, j + step) for j in range(0, PACK, step)]
 
         def load_chunk(i):
@@ -141,8 +142,7 @@ def tile_patternlayer_v_kernel(tc, inputs, train_data, dist, grad_out, out):
         def round_and_regroup(i):
             blk = chunks[i][0]
             e16[i] = work.tile([P, WIDTHS[blk], PACK], BF16, name="e16", align_bytes=64)
-            for n_cols in parts(blk):
-                regroup(nc.scalar.copy, e16[i][:, n_cols, :], e32[i][:, :, n_cols])
+            regroup(nc.scalar.copy, e16[i][:], e32[i][:])
 
         def regroup_x(c):
             for h in range(HALVES):
@@ -280,7 +280,7 @@ def tile_patternlayer_v_kernel(tc, inputs, train_data, dist, grad_out, out):
                 add_columns(k)
             for blk, t, h in leaving(k, True):
                 finish(blk, t, h)
-            for i in range(len(g_kept), min(k + (1 if k < 2 * PASSES else 2), LAST) + 1):
+            for i in range(len(g_kept), min(k + (1 if k < HALVED else 2), LAST) + 1):
                 for js in slots(i):
                     mask(i, js)
             if k == 0:

@@ -213,7 +213,7 @@ def tile_patternlayer_v_kernel(tc, inputs, train_data, dist, grad_out, out):
                 op1=ALU.add,
             )
             n_rows = slice(STARTS[blk] + t * P, STARTS[blk] + (t + 1) * P)
-            if blk == len(WIDTHS) - 1 and t == WIDTHS[blk] // P - 1:
+            if blk == len(WIDTHS) - 1 or (blk == len(WIDTHS) - 2 and t > 0):
                 nc.sync.dma_start(out=out[n_rows, halves[h]], in_=res[blk, t][:, halves[h]])
             elif h == HALVES - 1:
                 nc.sync.dma_start(out=out[n_rows, :], in_=res[blk, t][:])
@@ -249,7 +249,8 @@ def tile_patternlayer_v_kernel(tc, inputs, train_data, dist, grad_out, out):
             for blk in range(len(WIDTHS)):
                 for t, h in sums_of(blk):
                     held = blk == len(WIDTHS) - 2 and t > 0
-                    if held == late and k == (LAST + t - 1 if held else PASSES * (blk + 1) + 1):
+                    spare = blk == len(WIDTHS) - 3 and (t, h) in sums_of(blk)[BANKS:]
+                    if held == late and k == (LAST + t - 1 if held else PASSES * (blk + (2 if spare else 1)) + 1):
                         found.append((blk, t, h))
             return found
 

from contextlib import ExitStack

import concourse.mybir as mybir
from concourse.masks import make_identity

F32 = mybir.dt.float32
BF16 = mybir.dt.bfloat16
U32 = mybir.dt.uint32
U8 = mybir.dt.uint8
E4M3X4 = mybir.dt.float8_e4m3fn_x4
E5M2X4 = mybir.dt.float8_e5m2_x4
ALU = mybir.AluOpType
EXP = mybir.ActivationFunctionType.Exp
COPY = mybir.ActivationFunctionType.Copy

TOKENS, PATTERNS, FEATURES = 2560, 1536, 1024
FLOPS = 2 * TOKENS * PATTERNS * FEATURES

P = 128
PACK = 4
K_PASS = P * PACK
PASSES = TOKENS // K_PASS
WIDTHS = (512, 512, 384, 128)
STARTS = (0, 512, 1024, 1408)
LAST = len(WIDTHS) * PASSES - 1
HALF = 512
HALVES = FEATURES // HALF
RUN = 4
LOAD_BUFS = 4
LOAD_AHEAD = LOAD_BUFS
HALVED = 5
HEAD_CHUNKS = 1
PATTERNS_PASS = 1
BANKS = 7
PART = 256


def regroup(copy, grouped, rows):
    copy(
        out=grouped.rearrange("p (q i) j -> p q j i", i=RUN),
        in_=rows.rearrange("p j (q i) -> p q j i", i=RUN),
    )


def tile_patternlayer_v_kernel(tc, inputs, train_data, dist, grad_out, out):
    nc = tc.nc
    with ExitStack() as ctx:
        keep = ctx.enter_context(tc.tile_pool(name="keep", bufs=1))
        loads = ctx.enter_context(tc.tile_pool(name="loads", bufs=LOAD_BUFS))
        work = ctx.enter_context(tc.tile_pool(name="work", bufs=2))
        coded = ctx.enter_context(tc.tile_pool(name="coded", bufs=PASSES + 1))
        x_stage = ctx.enter_context(tc.tile_pool(name="x_stage", bufs=PASSES))
        t_pool = ctx.enter_context(tc.tile_pool(name="t_pool", bufs=2))
        results = ctx.enter_context(tc.tile_pool(name="results", bufs=4))
        acc_pool = ctx.enter_context(tc.psum_pool(name="acc_pool", bufs=BANKS))
        col_pool = ctx.enter_context(tc.psum_pool(name="col_pool", bufs=1))
        ctx.enter_context(tc.manual_schedule())

        identity = keep.tile([P, P], F32)
        make_identity(nc, identity[:])
        x_codes = keep.tile([P, PASSES, FEATURES], U32, align_bytes=64)
        x_scales = keep.tile([P, PASSES, FEATURES], U8, align_bytes=64)

        r, g, prob, g_kept, e32, e16 = {}, {}, {}, {}, {}, {}
        x_raw, x_grp, t_sb, col_ps, neg_col, acc = {}, {}, {}, {}, {}, {}
        e_codes, e_scales, res = {}, {}, {}
        halves = [slice(h * HALF, (h + 1) * HALF) for h in range(HALVES)]
        chunks = [(blk, c) for blk in range(len(WIDTHS)) for c in range(PASSES)]

        def tile_cols(t):
            return slice(t * P, (t + 1) * P)

        def sums_of(blk):
            return [(t, h) for t in range(WIDTHS[blk] // P) for h in range(HALVES)]

        def parts(blk):
            return [slice(n0, min(n0 + PART, WIDTHS[blk])) for n0 in range(0, WIDTHS[blk], PART)]

        def slots(i):
            step = 1 if i < HEAD_CHUNKS else 2 if i <= HALVED else PACK
            return [slice(j, j + step) for j in range(0, PACK, step)]

        def load_chunk(i):
            blk, c = chunks[i]
            rows = slice(c * K_PASS, (c + 1) * K_PASS)
            cols = slice(STARTS[blk], STARTS[blk] + WIDTHS[blk])
            r[i] = loads.tile([P, PACK, WIDTHS[blk]], F32, name="r")
            g[i] = loads.tile([P, PACK, WIDTHS[blk]], BF16, name="g")
            for js in slots(i) if i < HEAD_CHUNKS else [slice(0, PACK)]:
                nc.sync.dma_start(out=r[i][:, js, :], in_=dist[rows, cols].rearrange("(p j) n -> p j n", j=PACK)[:, js, :])
                nc.sync.dma_start(out=g[i][:, js, :], in_=grad_out[rows, cols].rearrange("(p j) n -> p j n", j=PACK)[:, js, :])

        def load_x(c):
            rows = inputs[c * K_PASS : (c + 1) * K_PASS, :].rearrange("(p j) d -> p j d", j=PACK)
            whole = x_stage.tile([P, PACK, FEATURES], BF16, name="x_raw")
            nc.sync.dma_start(out=whole[:], in_=rows)
            for h in range(HALVES):
                x_raw[c, h] = whole[:, :, halves[h]]

        def load_patterns(blk):
            t_sb[blk] = t_pool.tile([P, WIDTHS[blk] // P, FEATURES], BF16, name="t_sb")
            nc.sync.dma_start(
                out=t_sb[blk][:],
                in_=train_data[STARTS[blk] : STARTS[blk] + WIDTHS[blk], :].rearrange("(t p) d -> p t d", p=P),
            )

        def exponential(i, js):
            if i not in prob:
                prob[i] = work.tile([P, PACK, WIDTHS[chunks[i][0]]], F32, name="prob")
            nc.scalar.activation(out=prob[i][:, js, :], in_=r[i][:, js, :], func=EXP, scale=-0.5)

        def mask(i, js):
            if i not in g_kept:
                g_kept[i] = work.tile([P, PACK, WIDTHS[chunks[i][0]]], BF16, name="g_kept", bufs=3)
            nc.vector.scalar_tensor_tensor(
                out=g_kept[i][:, js, :], in0=r[i][:, js, :], scalar=0.0, in1=g[i][:, js, :], op0=ALU.is_gt, op1=ALU.mult
            )

        def times(i, js):
            if i not in e32:
                e32[i] = work.tile([P, PACK, WIDTHS[chunks[i][0]]], F32, name="e32")
            nc.vector.scalar_tensor_tensor(
                out=e32[i][:, js, :], in0=prob[i][:, js, :], scalar=1.0, in1=g_kept[i][:, js, :], op0=ALU.min, op1=ALU.mult
            )

        def add_columns(i):
            blk, c = chunks[i]
            n_tiles = WIDTHS[blk] // P
            if c == 0:
                col_ps[blk] = col_pool.tile([P, HALF], F32, name="col_ps")
            for t in range(n_tiles):
                for j in range(PACK):
                    nc.tensor.matmul(
                        out=col_ps[blk][:, tile_cols(t)],
                        lhsT=e32[i][:, j, tile_cols(t)],
                        rhs=identity[:],
                        is_transpose=True,
                        start=(c == 0 and t == 0 and j == 0),
                        stop=(c == PASSES - 1 and t == n_tiles - 1 and j == PACK - 1),
                    )

        def round_and_regroup(i):
            blk = chunks[i][0]
            e16[i] = work.tile([P, WIDTHS[blk], PACK], BF16, name="e16", align_bytes=64)
            regroup(nc.scalar.copy, e16[i][:], e32[i][:])

        def regroup_x(c):
            for h in range(HALVES):
                x_grp[c, h] = x_stage.tile(
                    [P, HALF, PACK], BF16, name="x_grp_s" if h == 0 else "x_grp_v", align_bytes=64, bufs=3 if h == 0 else 2
                )
                regroup(nc.scalar.copy if h == 0 else nc.vector.tensor_copy, x_grp[c, h][:], x_raw[c, h][:, :, :])

        def quantise_x(c, h):
            nc.vector.quantize_mx(
                out=x_codes[:, c, halves[h]].bitcast(E4M3X4),
                scales=x_scales[:, c, halves[h]],
                in_=x_grp[c, h][:].rearrange("p d j -> p (d j)"),
            )

        def multiply(blk, c, t, h):
            nc.tensor.matmul_mx(
                out=acc[blk, t, h][:],
                lhsT=e_codes[blk, c][:, tile_cols(t)].bitcast(E5M2X4),
                lhsT_scale=e_scales[blk, c][:, tile_cols(t)],
                rhs=x_codes[:, c, halves[h]].bitcast(E4M3X4),
                rhs_scale=x_scales[:, c, halves[h]],
                start=(c == 0),
                stop=(c == PASSES - 1),
            )

        def quantise_e(i):
            blk, c = chunks[i]
            e_codes[blk, c] = coded.tile([P, WIDTHS[blk]], U32, name="e_codes", align_bytes=64)
            e_scales[blk, c] = coded.tile([P, WIDTHS[blk]], U8, name="e_scales", align_bytes=64)
            for n_cols in [slice(0, WIDTHS[blk])] if WIDTHS[blk] in (P, 2 * P, 4 * P) else parts(blk):
                nc.vector.quantize_mx(
                    out=e_codes[blk, c][:, n_cols].bitcast(E5M2X4),
                    scales=e_scales[blk, c][:, n_cols],
                    in_=e16[i][:, n_cols, :].rearrange("p n j -> p (n j)"),
                )

        def multiply_chunk(i):
            blk, c = chunks[i]
            if c == 0:
                for t, h in sums_of(blk)[:BANKS]:
                    acc[blk, t, h] = acc_pool.tile([P, HALF], F32, name="acc")
            for t, h in sums_of(blk)[:BANKS]:
                multiply(blk, c, t, h)

        def sum_columns(blk):
            n_tiles = WIDTHS[blk] // P
            neg_col[blk] = results.tile([P, n_tiles], F32, name="neg_col", bufs=2)
            unread = results.tile([P, n_tiles, P], BF16, bufs=2)
            for t in range(n_tiles):
                nc.scalar.activation(
                    out=unread[:, t, :],
                    in_=col_ps[blk][:, tile_cols(t)],
                    func=COPY,
                    scale=-1.0,
                    accum_out=neg_col[blk][:, t : t + 1],
                )

        def finish(blk, t, h):
            if h == 0:
                res[blk, t] = results.tile([P, FEATURES], F32, name="res")
            nc.vector.scalar_tensor_tensor(
                out=res[blk, t][:, halves[h]],
                in0=t_sb[blk][:, t, halves[h]],
                scalar=neg_col[blk][:, t : t + 1],
                in1=acc[blk, t, h][:],
                op0=ALU.mult,
                op1=ALU.add,
            )
            n_rows = slice(STARTS[blk] + t * P, STARTS[blk] + (t + 1) * P)
            if blk == len(WIDTHS) - 1 or (blk == len(WIDTHS) - 2 and t > 0):
                nc.sync.dma_start(out=out[n_rows, halves[h]], in_=res[blk, t][:, halves[h]])
            elif h == HALVES - 1:
                nc.sync.dma_start(out=out[n_rows, :], in_=res[blk, t][:])
            if (t, h) == (0, 0):
                for t_late, h_late in sums_of(blk)[BANKS:]:
                    acc[blk, t_late, h_late] = acc_pool.tile([P, HALF], F32, name="acc")
                    for c in range(PASSES):
                        multiply(blk, c, t_late, h_late)

        load_chunk(0)
        for c in range(PASSES):
            load_x(c)
        for i in range(1, LOAD_AHEAD):
            load_chunk(i)
        for j, js in enumerate(slots(0)):
            exponential(0, js)
            mask(0, js)
            if j > 0:
                times(0, slots(0)[j - 1])
        times(0, slots(0)[-1])
        add_columns(0)
        round_and_regroup(0)
        for c in range(PASSES + 1):
            if c < PASSES:
                regroup_x(c)
            if c >= 1:
                quantise_x(c - 1, 1)
            if c >= 2:
                quantise_x(c - 2, 0)

        def leaving(k, late):
            found = []
            for blk in range(len(WIDTHS)):
                for t, h in sums_of(blk):
                    held = blk == len(WIDTHS) - 2 and t > 0
                    spare = blk == len(WIDTHS) - 3 and (t, h) in sums_of(blk)[BANKS:]
                    if held == late and k == (LAST + t - 1 if held else PASSES * (blk + (2 if spare else 1)) + 1):
                        found.append((blk, t, h))
            return found

        for k in range(len(chunks) + 2):
            if k + LOAD_AHEAD <= LAST:
                load_chunk(k + LOAD_AHEAD)
            if k <= LAST and chunks[k][1] == PATTERNS_PASS:
                load_patterns(chunks[k][0])
            if k + 1 <= LAST:
                for js in slots(k + 1):
                    exponential(k + 1, js)
            if k >= PASSES and k % PASSES == 0:
                sum_columns(k // PASSES - 1)
            if 1 <= k <= LAST:
                for js in slots(k):
                    times(k, js)
            passes_first = k <= 2 * PASSES or k % PASSES == 0
            if k <= LAST and not passes_first:
                add_columns(k)
            if 1 <= k <= LAST:
                round_and_regroup(k)
            for blk, t, h in leaving(k, False):
                finish(blk, t, h)
            if 1 <= k <= LAST + 1:
                quantise_e(k - 1)
                multiply_chunk(k - 1)
            if 1 <= k <= LAST and passes_first:
                add_columns(k)
            for blk, t, h in leaving(k, True):
                finish(blk, t, h)
            for i in range(len(g_kept), min(k + (1 if k < HALVED else 2), LAST) + 1):
                for js in slots(i):
                    mask(i, js)
            if k == 0:
                quantise_x(PASSES - 1, 0)
